import numpy as np
import ml_dtypes


def mxq(x, axis, fmt="e4m3"):
    dtype, down = {"e4m3": (ml_dtypes.float8_e4m3fn, 7), "e5m2": (ml_dtypes.float8_e5m2, 14)}[fmt]
    v = np.moveaxis(np.asarray(x, np.float32).astype(ml_dtypes.bfloat16).astype(np.float64), axis, -1)
    blocks = v.reshape(v.shape[:-1] + (-1, 32))
    amax = np.abs(blocks).max(-1, keepdims=True)
    byte = np.maximum(np.where(amax > 0, np.frexp(amax)[1] - 1 + 127, 0) - down, 1)
    scale = np.exp2(byte - 127.0)
    codes = (blocks / scale).astype(np.float32).astype(dtype).astype(np.float64)
    return np.moveaxis((codes * scale).reshape(v.shape), -1, axis)


WIDE = False


def mx_kscale(k):
    if not WIDE:
        return np.ones(k)
    levels = np.array([10, -10, 5, -5, 0])
    if k % 512:
        return np.exp2(np.random.permutation(np.resize(levels, k // 32))).repeat(32)
    a = np.empty((k // 512, 16))
    for p in range(k // 512):
        a[p, :8] = np.random.permutation(np.resize(levels, 8))
        for g in range(8):
            far = levels[np.abs(levels - a[p, g]) >= 10]
            a[p, g + 8] = far[np.random.randint(len(far))]
    return np.exp2(a.ravel()).repeat(32)


BF16 = ml_dtypes.bfloat16


def bf(x):
    return np.asarray(x, np.float32).astype(BF16)


def f64(x):
    return np.asarray(x).astype(np.float64)


N, H, O, L = 1024, 512, 512, 4


def represent(h):
    n = h.shape[0]
    total = np.sum(h, axis=0, keepdims=True)
    return (n * h - total) / (n - 1)


def sigmoid(v):
    return 1.0 / (1.0 + np.exp(-v))


def setup_inputs():
    t = mx_kscale(H)
    mu = np.random.standard_normal(H)
    return {"h": bf((np.random.standard_normal((N, H)) * 1.2 + mu) * t),
            "w": bf(np.random.standard_normal((H, H)) * 0.6 / np.sqrt(H) * t[:, None] / t[None, :]),
            "w_ff": bf(np.random.standard_normal((O, H)) * 0.6 / np.sqrt(H) / t[None, :]),
            "b_ff": bf(np.random.standard_normal(O) * 0.3)}


def reference(h, w, w_ff, b_ff):
    h = f64(h)
    r = represent(h)
    f = f64(bf(mxq(r, 1, "e4m3") @ mxq(f64(w), 1, "e4m3").T))
    h_new = f + h
    return sigmoid((mxq(h_new, 1, "e4m3") @ mxq(f64(w_ff), 1, "e4m3").T) + f64(b_ff))

@@ -1,0 +1,324 @@
+from contextlib import ExitStack
+
+import concourse.mybir as mybir
+from concourse.masks import make_identity
+
+N_ROWS, H, O = 1024, 512, 512
+FLOPS = 2 * N_ROWS * H * H + 2 * N_ROWS * H * O
+
+F32 = mybir.dt.float32
+BF16 = mybir.dt.bfloat16
+U32 = mybir.dt.uint32
+U8 = mybir.dt.uint8
+FP8X4 = mybir.dt.float8_e4m3fn_x4
+ALU = mybir.AluOpType
+ACT = mybir.ActivationFunctionType
+AX = mybir.AxisListType
+
+P = 128
+NT = N_ROWS // P
+BANK1 = BF16
+
+
+def tile_differ_amplifier_pa_kernel(tc, h, w, w_ff, b_ff, out):
+    nc = tc.nc
+    with ExitStack() as ctx:
+        const = ctx.enter_context(tc.tile_pool(name="const", bufs=1))
+        keep = ctx.enter_context(tc.tile_pool(name="keep", bufs=1))
+        work = ctx.enter_context(tc.tile_pool(name="work", bufs=8))
+        psum = ctx.enter_context(tc.psum_pool(name="psum", bufs=8))
+        ctx.enter_context(tc.manual_schedule())
+
+        h_v = h.rearrange("(p i) k -> p i k", i=NT)
+        out_v = out.rearrange("(p i) o -> p i o", i=NT)
+        w_v = w.rearrange("(j m) k -> m j k", j=4)
+        wff_v = w_ff.rearrange("(j m) k -> m j k", j=4)
+
+        h_nat = []
+        for j in range(4):
+            t = keep.tile([P, 2, H], BF16, name="h_nat%d" % j)
+            nc.sync.dma_start(out=t[:], in_=h_v[:, 2 * j : 2 * j + 2, :])
+            h_nat.append(t)
+        w_nat = []
+        for b in range(2):
+            t = keep.tile([P, 2, H], BF16, name="w_nat%d" % b)
+            nc.sync.dma_start(out=t[:], in_=w_v[:, 2 * b : 2 * b + 2, :])
+            w_nat.append(t)
+        wff_nat = []
+        for b in range(2):
+            t = keep.tile([P, 2, H], BF16, name="wff_nat%d" % b)
+            nc.sync.dma_start(out=t[:], in_=wff_v[:, 2 * b : 2 * b + 2, :])
+            wff_nat.append(t)
+
+        ones = const.tile([P, P], BF16, name="ones")
+        nc.vector.memset(ones[:], 1.0)
+
+        ident = const.tile([P, P], F32, name="ident")
+        make_identity(nc, ident[:])
+        brow = const.tile([P, O], BF16, name="brow")
+        nc.vector.memset(brow[:], 0.0)
+        nc.scalar.dma_start(out=brow[0:1, :], in_=b_ff.rearrange("(a o) -> a o", a=1))
+        warm = const.tile([P, 1], F32, name="warm")
+        nc.vector.memset(warm[:], 0.0)
+        nc.scalar.activation(out=warm[:], in_=warm[:], func=ACT.Sigmoid)
+
+
+        def transpose_words(bank, src_bf16):
+            words = src_bf16.bitcast(F32)
+            for u in range(2):
+                nc.tensor.transpose(bank[:, u, :], words[:, u : H // 2 : 2], ident[:])
+
+        tot_ps = psum.tile([P, 4, NT], F32, tag="bank", name="tot_ps")
+        hI = [None] * 4
+
+        def totals(j):
+            for ii in range(2):
+                i = 2 * j + ii
+                for t in range(4):
+                    nc.tensor.matmul(
+                        tot_ps[:, t, i : i + 1],
+                        lhsT=h_nat[j][:, ii, t:H:4],
+                        rhs=ones[:, 0:1],
+                        start=True,
+                        stop=True,
+                    )
+
+        tp_h = [None] * 4
+
+        def th(j):
+            tp_h[j] = psum.tile([P, 2, 2, P], F32, tag="bank", name="tp_h")
+            for ii in range(2):
+                transpose_words(tp_h[j][:, ii], h_nat[j][:, ii, :])
+
+        def hi(j):
+            hI[j] = keep.tile([P, 2 * P * 4], BF16, name="hI%d" % j, align_bytes=64)
+            nc.scalar.copy(
+                out=hI[j][:].bitcast(F32).rearrange("p (i n u) -> p i n u", i=2, u=2),
+                in_=tp_h[j][:].rearrange("p i u n -> p i n u"),
+            )
+
+        def weight_tiles(label):
+            grouped = keep.tile([P, O * 4], BF16, name=label + "_I", align_bytes=64)
+            codes = keep.tile([P, O], U32, name=label + "_codes", align_bytes=64)
+            scales = keep.tile([P, O], U8, name=label + "_scales", align_bytes=64)
+            return grouped, codes, scales
+
+        tp_w = {}
+
+        def tw(label, nat, b):
+            tp_w[(label, b)] = psum.tile([P, 2, 2, P], F32, tag="bank", name="tp_w")
+            for jj in range(2):
+                transpose_words(tp_w[(label, b)][:, jj], nat[b][:, jj, :])
+
+        def cw(label, grouped, b):
+            dst = grouped[:, b * 1024 : (b + 1) * 1024].bitcast(F32)
+            nc.scalar.copy(
+                out=dst.rearrange("p (j m u) -> p j m u", j=2, u=2),
+                in_=tp_w[(label, b)][:].rearrange("p j u m -> p j m u"),
+            )
+
+        def quant_weight(grouped, codes, scales, b):
+            nc.vector.quantize_mx(
+                out=codes[:, b * 256 : (b + 1) * 256].bitcast(FP8X4),
+                scales=scales[:, b * 256 : (b + 1) * 256],
+                in_=grouped[:, b * 1024 : (b + 1) * 1024],
+            )
+
+        w_I, w_codes, w_scales = weight_tiles("w")
+        wff_I, wff_codes, wff_scales = weight_tiles("wff")
+        tot = const.tile([P, 4], F32, name="tot")
+        cmean = const.tile([P, 4], F32, name="cmean")
+        biasB = const.tile([P, O], F32, name="biasB")
+
+        rI = []
+        r_codes = []
+        r_scales = []
+        hnI = []
+        hn_codes = []
+        hn_scales = []
+        for half in range(2):
+            rI.append(keep.tile([P, 2048], BF16, name="rI%d" % half, align_bytes=64))
+            r_codes.append(keep.tile([P, 512], U32, name="r_codes%d" % half, align_bytes=64))
+            r_scales.append(keep.tile([P, 512], U8, name="r_scales%d" % half, align_bytes=64))
+            hnI.append(keep.tile([P, 2048], BF16, name="hnI%d" % half, align_bytes=64))
+            hn_codes.append(keep.tile([P, 512], U32, name="hn_codes%d" % half, align_bytes=64))
+            hn_scales.append(keep.tile([P, 512], U8, name="hn_scales%d" % half, align_bytes=64))
+        s1 = [None] * NT
+        hn = [None] * NT
+        tp_hn = [None] * NT
+        s2 = [None] * NT
+        pre = [None] * NT
+
+        def st_a(j):
+            nc.vector.scalar_tensor_tensor(
+                out=rI[j // 2][:, (j % 2) * 1024 : (j % 2 + 1) * 1024].rearrange("p (n t) -> p n t", t=4),
+                in0=hI[j][:].rearrange("p (n t) -> p n t", t=4),
+                scalar=float(N_ROWS) / (N_ROWS - 1),
+                in1=cmean[:].unsqueeze(1).to_broadcast([P, 2 * P, 4]),
+                op0=ALU.mult,
+                op1=ALU.subtract,
+            )
+
+        def st_b(half):
+            nc.vector.quantize_mx(
+                out=r_codes[half][:].bitcast(FP8X4), scales=r_scales[half][:], in_=rI[half][:]
+            )
+
+        def st_c(i):
+            half, q = i // 4, i % 4
+            s1[i] = psum.tile([P, H], BANK1, tag="bank", name="s1")
+            nc.tensor.matmul_mx(
+                out=s1[i][:],
+                lhsT=r_codes[half][:, q * P : (q + 1) * P].bitcast(FP8X4),
+                lhsT_scale=r_scales[half][:, q * P : (q + 1) * P],
+                rhs=w_codes[:].bitcast(FP8X4),
+                rhs_scale=w_scales[:],
+                start=True,
+                stop=True,
+            )
+
+        def st_d(i):
+            hn[i] = work.tile([P, H], BF16, name="hn")
+            nc.vector.tensor_tensor(out=hn[i][:], in0=s1[i][:], in1=h_nat[i // 2][:, i % 2, :], op=ALU.add)
+
+        def st_e(i):
+            tp_hn[i] = psum.tile([P, 2, P], F32, tag="bank", name="tp_hn")
+            transpose_words(tp_hn[i], hn[i][:])
+
+        def st_f(i):
+            half, q = i // 4, i % 4
+            nc.scalar.copy(
+                out=hnI[half][:, q * 512 : (q + 1) * 512].bitcast(F32).rearrange("p (n u) -> p n u", u=2),
+                in_=tp_hn[i][:].rearrange("p u n -> p n u"),
+            )
+
+        def st_g(part):
+            half, lo, hi_ = {0: (0, 0, 4), 1: (1, 0, 4), 8: (1, 0, 2), 9: (1, 2, 4)}[part]
+            nc.vector.quantize_mx(
+                out=hn_codes[half][:, lo * P : hi_ * P].bitcast(FP8X4),
+                scales=hn_scales[half][:, lo * P : hi_ * P],
+                in_=hnI[half][:, lo * 4 * P : hi_ * 4 * P],
+            )
+
+        def st_h(i):
+            half, q = i // 4, i % 4
+            s2[i] = psum.tile([P, O], F32, tag="bank", name="s2")
+            nc.tensor.matmul_mx(
+                out=s2[i][:],
+                lhsT=hn_codes[half][:, q * P : (q + 1) * P].bitcast(FP8X4),
+                lhsT_scale=hn_scales[half][:, q * P : (q + 1) * P],
+                rhs=wff_codes[:].bitcast(FP8X4),
+                rhs_scale=wff_scales[:],
+                start=True,
+                stop=True,
+            )
+
+        res = [None] * NT
+
+        def st_i(i, lo=0, hi_=O):
+            if lo == 0:
+                pre[i] = work.tile([P, O], F32, name="pre")
+            nc.vector.tensor_tensor(out=pre[i][:, lo:hi_], in0=s2[i][:, lo:hi_], in1=biasB[:, lo:hi_], op=ALU.add)
+
+        def st_j(i, lo=0, hi_=O):
+            if lo == 0:
+                res[i] = work.tile([P, O], F32, name="res")
+            nc.scalar.activation(out=res[i][:, lo:hi_], in_=pre[i][:, lo:hi_], func=ACT.Sigmoid)
+            nc.sync.dma_start(out=out_v[:, i, lo:hi_], in_=res[i][:, lo:hi_])
+
+        totals(0)
+        th(0)
+        hi(0)
+        totals(1)
+        totals(2)
+        totals(3)
+        nc.vector.tensor_reduce(out=tot[:], in_=tot_ps[:], axis=AX.X, op=ALU.add)
+        nc.vector.tensor_scalar_mul(cmean[:], tot[:], 1.0 / (N_ROWS - 1))
+        th(1)
+        hi(1)
+        tw("w", w_nat, 0)
+        cw("w", w_I, 0)
+        tw("w", w_nat, 1)
+        cw("w", w_I, 1)
+        th(2)
+        hi(2)
+        th(3)
+        hi(3)
+        bias_ps = psum.tile([P, O], F32, tag="bank", name="bias_ps")
+        nc.tensor.matmul(bias_ps[:], lhsT=ones[:], rhs=brow[:], start=True, stop=True)
+        nc.scalar.copy(out=biasB[:], in_=bias_ps[:])
+        tw("wff", wff_nat, 0)
+        cw("wff", wff_I, 0)
+        tw("wff", wff_nat, 1)
+        cw("wff", wff_I, 1)
+        st_a(0)
+        st_a(1)
+        quant_weight(w_I, w_codes, w_scales, 0)
+        quant_weight(w_I, w_codes, w_scales, 1)
+        st_b(0)
+        st_c(0)
+        st_c(1)
+        st_c(2)
+        st_c(3)
+        st_a(2)
+        st_d(0)
+        st_e(0)
+        st_f(0)
+        st_d(1)
+        st_e(1)
+        st_f(1)
+        st_a(3)
+        st_d(2)
+        st_e(2)
+        st_f(2)
+        st_d(3)
+        st_e(3)
+        st_f(3)
+        st_b(1)
+        st_c(4)
+        st_c(5)
+        st_c(6)
+        st_c(7)
+        quant_weight(wff_I, wff_codes, wff_scales, 0)
+        quant_weight(wff_I, wff_codes, wff_scales, 1)
+        st_g(0)
+        st_h(0)
+        st_h(1)
+        st_h(2)
+        st_h(3)
+        st_d(4)
+        st_e(4)
+        st_f(4)
+        st_d(5)
+        st_e(5)
+        st_f(5)
+        st_d(6)
+        st_e(6)
+        st_f(6)
+        st_d(7)
+        st_e(7)
+        st_f(7)
+        st_i(0)
+        st_j(0)
+        st_i(1)
+        st_j(1)
+        st_i(2)
+        st_j(2)
+        st_g(8)
+        st_h(4)
+        st_h(5)
+        st_i(3)
+        st_j(3)
+        st_g(9)
+        st_h(6)
+        st_h(7)
+        st_i(4)
+        st_j(4)
+        st_i(5)
+        st_j(5)
+        st_i(6)
+        st_j(6)
+        st_i(7, 0, 256)
+        st_j(7, 0, 256)
+        st_i(7, 256, 512)
+        st_j(7, 256, 512)

@@ -68,19 +68,20 @@ def tile_differ_amplifier_pa_kernel(tc, h, w, w_ff, b_ff, out):
             for u in range(2):
                 nc.tensor.transpose(bank[:, u, :], words[:, u : H // 2 : 2], ident[:])
 
-        tot_ps = psum.tile([P, 4, NT], F32, tag="bank", name="tot_ps")
+        tot_a = psum.tile([P, 4, 3], F32, tag="bank", name="tot_a")
+        tot_b = psum.tile([P, 4, 1], F32, tag="bank", name="tot_b")
         hI = [None] * 4
 
         def totals(j):
-            for ii in range(2):
-                i = 2 * j + ii
-                for t in range(4):
+            dst = tot_a[:, :, j : j + 1] if j < 3 else tot_b
+            for t in range(4):
+                for ii in range(2):
                     nc.tensor.matmul(
-                        tot_ps[:, t, i : i + 1],
+                        dst[:, t, :],
                         lhsT=h_nat[j][:, ii, t:H:4],
                         rhs=ones[:, 0:1],
-                        start=True,
-                        stop=True,
+                        start=(ii == 0),
+                        stop=(ii == 1),
                     )
 
         tp_h = [None] * 4
@@ -127,7 +128,8 @@ def tile_differ_amplifier_pa_kernel(tc, h, w, w_ff, b_ff, out):
         w_I, w_codes, w_scales = weight_tiles("w")
         wff_I, wff_codes, wff_scales = weight_tiles("wff")
         tot = const.tile([P, 4], F32, name="tot")
-        cmean = const.tile([P, 4], F32, name="cmean")
+        part = const.tile([P, 4], F32, name="part")
+        negc = const.tile([P, 4], F32, name="negc")
         biasB = const.tile([P, O], F32, name="biasB")
 
         rI = []
@@ -149,15 +151,30 @@ def tile_differ_amplifier_pa_kernel(tc, h, w, w_ff, b_ff, out):
         s2 = [None] * NT
         pre = [None] * NT
 
-        def st_a(j):
+        A_SCALE = float(N_ROWS) / (N_ROWS - 1)
+
+        def st_a(j, tiles=2):
+            lo = (j % 2) * 1024
             nc.vector.scalar_tensor_tensor(
-                out=rI[j // 2][:, (j % 2) * 1024 : (j % 2 + 1) * 1024].rearrange("p (n t) -> p n t", t=4),
-                in0=hI[j][:].rearrange("p (n t) -> p n t", t=4),
-                scalar=float(N_ROWS) / (N_ROWS - 1),
-                in1=cmean[:].unsqueeze(1).to_broadcast([P, 2 * P, 4]),
+                out=rI[j // 2][:, lo : lo + tiles * 512].rearrange("p (n t) -> p n t", t=4),
+                in0=hI[j][:, 0 : tiles * 512].rearrange("p (n t) -> p n t", t=4),
+                scalar=A_SCALE,
+                in1=negc[:].unsqueeze(1).to_broadcast([P, tiles * P, 4]),
                 op0=ALU.mult,
-                op1=ALU.subtract,
+                op1=ALU.add,
             )
+
+        def st_z(i):
+            j, lo = i // 2, (i % 2) * 512
+            dst = rI[j // 2][:, (j % 2) * 1024 + lo : (j % 2) * 1024 + lo + 512]
+            for t in range(4):
+                nc.scalar.activation(
+                    out=dst[:, t:512:4],
+                    in_=hI[j][:, lo + t : lo + 512 : 4],
+                    func=ACT.Identity,
+                    bias=negc[:, t : t + 1],
+                    scale=A_SCALE,
+                )
 
         def st_b(half):
             nc.vector.quantize_mx(
@@ -231,9 +248,17 @@ def tile_differ_amplifier_pa_kernel(tc, h, w, w_ff, b_ff, out):
         hi(0)
         totals(1)
         totals(2)
+        nc.vector.tensor_reduce(out=tot[:], in_=tot_a[:], axis=AX.X, op=ALU.add)
+        nc.vector.tensor_scalar_mul(part[:], tot[:], -1.0 / (N_ROWS - 1))
         totals(3)
-        nc.vector.tensor_reduce(out=tot[:], in_=tot_ps[:], axis=AX.X, op=ALU.add)
-        nc.vector.tensor_scalar_mul(cmean[:], tot[:], 1.0 / (N_ROWS - 1))
+        nc.vector.scalar_tensor_tensor(
+            out=negc[:],
+            in0=tot_b[:, :, 0],
+            scalar=-1.0 / (N_ROWS - 1),
+            in1=part[:],
+            op0=ALU.mult,
+            op1=ALU.add,
+        )
         th(1)
         hi(1)
         tw("w", w_nat, 0)
@@ -261,13 +286,14 @@ def tile_differ_amplifier_pa_kernel(tc, h, w, w_ff, b_ff, out):
         st_c(2)
         st_c(3)
         st_a(2)
+        st_z(7)
         st_d(0)
         st_e(0)
         st_f(0)
         st_d(1)
         st_e(1)
         st_f(1)
-        st_a(3)
+        st_a(3, 1)
         st_d(2)
         st_e(2)
         st_f(2)

@@ -52,7 +52,8 @@ def tile_differ_amplifier_pa_kernel(tc, h, w, w_ff, b_ff, out):
 
         ones = const.tile([P, P], BF16, name="ones")
         nc.vector.memset(ones[:], 1.0)
-
+        junk = const.tile([P, O], BF16, name="junk")
+        nc.vector.memset(junk[:], 0.0)
         ident = const.tile([P, P], F32, name="ident")
         make_identity(nc, ident[:])
         brow = const.tile([P, O], BF16, name="brow")
@@ -62,26 +63,30 @@ def tile_differ_amplifier_pa_kernel(tc, h, w, w_ff, b_ff, out):
         nc.vector.memset(warm[:], 0.0)
         nc.scalar.activation(out=warm[:], in_=warm[:], func=ACT.Sigmoid)
 
+        warm_ps = psum.tile([P, O], F32, tag="bank", name="warm_ps")
+
+        def warm_up(count):
+            for rep in range(count):
+                nc.tensor.matmul(warm_ps[:], lhsT=ones[:], rhs=junk[:], start=True, stop=True)
 
         def transpose_words(bank, src_bf16):
             words = src_bf16.bitcast(F32)
             for u in range(2):
                 nc.tensor.transpose(bank[:, u, :], words[:, u : H // 2 : 2], ident[:])
 
-        tot_a = psum.tile([P, 4, 3], F32, tag="bank", name="tot_a")
-        tot_b = psum.tile([P, 4, 1], F32, tag="bank", name="tot_b")
+        tot_ps = psum.tile([P, 4, NT], F32, tag="bank", name="tot_ps")
         hI = [None] * 4
 
         def totals(j):
-            dst = tot_a[:, :, j : j + 1] if j < 3 else tot_b
-            for t in range(4):
-                for ii in range(2):
+            for ii in range(2):
+                i = 2 * j + ii
+                for t in range(4):
                     nc.tensor.matmul(
-                        dst[:, t, :],
+                        tot_ps[:, t, i : i + 1],
                         lhsT=h_nat[j][:, ii, t:H:4],
                         rhs=ones[:, 0:1],
-                        start=(ii == 0),
-                        stop=(ii == 1),
+                        start=True,
+                        stop=True,
                     )
 
         tp_h = [None] * 4
@@ -128,8 +133,7 @@ def tile_differ_amplifier_pa_kernel(tc, h, w, w_ff, b_ff, out):
         w_I, w_codes, w_scales = weight_tiles("w")
         wff_I, wff_codes, wff_scales = weight_tiles("wff")
         tot = const.tile([P, 4], F32, name="tot")
-        part = const.tile([P, 4], F32, name="part")
-        negc = const.tile([P, 4], F32, name="negc")
+        cmean = const.tile([P, 4], F32, name="cmean")
         biasB = const.tile([P, O], F32, name="biasB")
 
         rI = []
@@ -151,30 +155,15 @@ def tile_differ_amplifier_pa_kernel(tc, h, w, w_ff, b_ff, out):
         s2 = [None] * NT
         pre = [None] * NT
 
-        A_SCALE = float(N_ROWS) / (N_ROWS - 1)
-
-        def st_a(j, tiles=2):
-            lo = (j % 2) * 1024
+        def st_a(j):
             nc.vector.scalar_tensor_tensor(
-                out=rI[j // 2][:, lo : lo + tiles * 512].rearrange("p (n t) -> p n t", t=4),
-                in0=hI[j][:, 0 : tiles * 512].rearrange("p (n t) -> p n t", t=4),
-                scalar=A_SCALE,
-                in1=negc[:].unsqueeze(1).to_broadcast([P, tiles * P, 4]),
+                out=rI[j // 2][:, (j % 2) * 1024 : (j % 2 + 1) * 1024].rearrange("p (n t) -> p n t", t=4),
+                in0=hI[j][:].rearrange("p (n t) -> p n t", t=4),
+                scalar=float(N_ROWS) / (N_ROWS - 1),
+                in1=cmean[:].unsqueeze(1).to_broadcast([P, 2 * P, 4]),
                 op0=ALU.mult,
-                op1=ALU.add,
+                op1=ALU.subtract,
             )
-
-        def st_z(i):
-            j, lo = i // 2, (i % 2) * 512
-            dst = rI[j // 2][:, (j % 2) * 1024 + lo : (j % 2) * 1024 + lo + 512]
-            for t in range(4):
-                nc.scalar.activation(
-                    out=dst[:, t:512:4],
-                    in_=hI[j][:, lo + t : lo + 512 : 4],
-                    func=ACT.Identity,
-                    bias=negc[:, t : t + 1],
-                    scale=A_SCALE,
-                )
 
         def st_b(half):
             nc.vector.quantize_mx(
@@ -243,22 +232,15 @@ def tile_differ_amplifier_pa_kernel(tc, h, w, w_ff, b_ff, out):
             nc.scalar.activation(out=res[i][:, lo:hi_], in_=pre[i][:, lo:hi_], func=ACT.Sigmoid)
             nc.sync.dma_start(out=out_v[:, i, lo:hi_], in_=res[i][:, lo:hi_])
 
+        warm_up(3)
         totals(0)
         th(0)
         hi(0)
         totals(1)
         totals(2)
-        nc.vector.tensor_reduce(out=tot[:], in_=tot_a[:], axis=AX.X, op=ALU.add)
-        nc.vector.tensor_scalar_mul(part[:], tot[:], -1.0 / (N_ROWS - 1))
         totals(3)
-        nc.vector.scalar_tensor_tensor(
-            out=negc[:],
-            in0=tot_b[:, :, 0],
-            scalar=-1.0 / (N_ROWS - 1),
-            in1=part[:],
-            op0=ALU.mult,
-            op1=ALU.add,
-        )
+        nc.vector.tensor_reduce(out=tot[:], in_=tot_ps[:], axis=AX.X, op=ALU.add)
+        nc.vector.tensor_scalar_mul(cmean[:], tot[:], 1.0 / (N_ROWS - 1))
         th(1)
         hi(1)
         tw("w", w_nat, 0)
@@ -286,14 +268,13 @@ def tile_differ_amplifier_pa_kernel(tc, h, w, w_ff, b_ff, out):
         st_c(2)
         st_c(3)
         st_a(2)
-        st_z(7)
         st_d(0)
         st_e(0)
         st_f(0)
         st_d(1)
         st_e(1)
         st_f(1)
-        st_a(3, 1)
+        st_a(3)
         st_d(2)
         st_e(2)
         st_f(2)

@@ -162,7 +162,28 @@ def tile_differ_amplifier_pa_kernel(tc, h, w, w_ff, b_ff, out):
                 scalar=float(N_ROWS) / (N_ROWS - 1),
                 in1=cmean[:].unsqueeze(1).to_broadcast([P, 2 * P, 4]),
                 op0=ALU.mult,
-                op1=ALU.subtract,
+                op1=ALU.add,
+            )
+
+        rT = [None] * 4
+
+        def st_aS(j):
+            rT[j] = keep.tile([P, 4, 2, P], BF16, name="rT%d" % j)
+            halves = tp_h[j][:].bitcast(BF16).rearrange("p i u (n e) -> p i u n e", e=2)
+            for u in range(2):
+                for e in range(2):
+                    nc.scalar.activation(
+                        out=rT[j][:, 2 * u + e],
+                        in_=halves[:, :, u, :, e],
+                        func=ACT.Identity,
+                        scale=float(N_ROWS) / (N_ROWS - 1),
+                        bias=cmean[:, 2 * u + e : 2 * u + e + 1],
+                    )
+
+        def st_aV(j):
+            nc.vector.tensor_copy(
+                out=rI[j // 2][:, (j % 2) * 1024 : (j % 2 + 1) * 1024].rearrange("p (n t) -> p n t", t=4),
+                in_=rT[j][:].rearrange("p t i n -> p (i n) t"),
             )
 
         def st_b(half):
@@ -240,7 +261,7 @@ def tile_differ_amplifier_pa_kernel(tc, h, w, w_ff, b_ff, out):
         totals(2)
         totals(3)
         nc.vector.tensor_reduce(out=tot[:], in_=tot_ps[:], axis=AX.X, op=ALU.add)
-        nc.vector.tensor_scalar_mul(cmean[:], tot[:], 1.0 / (N_ROWS - 1))
+        nc.vector.tensor_scalar_mul(cmean[:], tot[:], -1.0 / (N_ROWS - 1))
         th(1)
         hi(1)
         tw("w", w_nat, 0)
@@ -248,12 +269,9 @@ def tile_differ_amplifier_pa_kernel(tc, h, w, w_ff, b_ff, out):
         tw("w", w_nat, 1)
         cw("w", w_I, 1)
         th(2)
-        hi(2)
+        st_aS(2)
         th(3)
-        hi(3)
-        bias_ps = psum.tile([P, O], F32, tag="bank", name="bias_ps")
-        nc.tensor.matmul(bias_ps[:], lhsT=ones[:], rhs=brow[:], start=True, stop=True)
-        nc.scalar.copy(out=biasB[:], in_=bias_ps[:])
+        st_aS(3)
         tw("wff", wff_nat, 0)
         cw("wff", wff_I, 0)
         tw("wff", wff_nat, 1)
@@ -267,20 +285,23 @@ def tile_differ_amplifier_pa_kernel(tc, h, w, w_ff, b_ff, out):
         st_c(1)
         st_c(2)
         st_c(3)
-        st_a(2)
+        st_aV(2)
         st_d(0)
         st_e(0)
         st_f(0)
         st_d(1)
         st_e(1)
         st_f(1)
-        st_a(3)
+        st_aV(3)
         st_d(2)
         st_e(2)
         st_f(2)
         st_d(3)
         st_e(3)
         st_f(3)
+        bias_ps = psum.tile([P, O], F32, tag="bank", name="bias_ps")
+        nc.tensor.matmul(bias_ps[:], lhsT=ones[:], rhs=brow[:], start=True, stop=True)
+        nc.scalar.copy(out=biasB[:], in_=bias_ps[:])
         st_b(1)
         st_c(4)
         st_c(5)

@@ -123,12 +123,8 @@ def tile_differ_amplifier_pa_kernel(tc, h, w, w_ff, b_ff, out):
                 in_=tp_w[(label, b)][:].rearrange("p j u m -> p j m u"),
             )
 
-        def quant_weight(grouped, codes, scales, b):
-            nc.vector.quantize_mx(
-                out=codes[:, b * 256 : (b + 1) * 256].bitcast(FP8X4),
-                scales=scales[:, b * 256 : (b + 1) * 256],
-                in_=grouped[:, b * 1024 : (b + 1) * 1024],
-            )
+        def quant_weight(grouped, codes, scales):
+            nc.vector.quantize_mx(out=codes[:].bitcast(FP8X4), scales=scales[:], in_=grouped[:])
 
         w_I, w_codes, w_scales = weight_tiles("w")
         wff_I, wff_codes, wff_scales = weight_tiles("wff")
@@ -149,9 +145,9 @@ def tile_differ_amplifier_pa_kernel(tc, h, w, w_ff, b_ff, out):
             hnI.append(keep.tile([P, 2048], BF16, name="hnI%d" % half, align_bytes=64))
             hn_codes.append(keep.tile([P, 512], U32, name="hn_codes%d" % half, align_bytes=64))
             hn_scales.append(keep.tile([P, 512], U8, name="hn_scales%d" % half, align_bytes=64))
-        s1 = [None] * NT
-        hn = [None] * NT
-        tp_hn = [None] * NT
+        s1 = [None] * 4
+        hn = [None] * 4
+        tp_hn = [None] * 4
         s2 = [None] * NT
         pre = [None] * NT
 
@@ -186,16 +182,20 @@ def tile_differ_amplifier_pa_kernel(tc, h, w, w_ff, b_ff, out):
                 in_=rT[j][:].rearrange("p t i n -> p (i n) t"),
             )
 
-        def st_b(half):
+        def st_b(j):
+            half, q = j // 2, j % 2
             nc.vector.quantize_mx(
-                out=r_codes[half][:].bitcast(FP8X4), scales=r_scales[half][:], in_=rI[half][:]
+                out=r_codes[half][:, q * 2 * P : (q + 1) * 2 * P].bitcast(FP8X4),
+                scales=r_scales[half][:, q * 2 * P : (q + 1) * 2 * P],
+                in_=rI[half][:, q * 1024 : (q + 1) * 1024],
             )
 
         def st_c(i):
             half, q = i // 4, i % 4
-            s1[i] = psum.tile([P, H], BANK1, tag="bank", name="s1")
+            if i % 2 == 0:
+                s1[i // 2] = psum.tile([P, 2, H], BANK1, tag="bank", name="s1")
             nc.tensor.matmul_mx(
-                out=s1[i][:],
+                out=s1[i // 2][:, i % 2, :],
                 lhsT=r_codes[half][:, q * P : (q + 1) * P].bitcast(FP8X4),
                 lhsT_scale=r_scales[half][:, q * P : (q + 1) * P],
                 rhs=w_codes[:].bitcast(FP8X4),
@@ -204,27 +204,28 @@ def tile_differ_amplifier_pa_kernel(tc, h, w, w_ff, b_ff, out):
                 stop=True,
             )
 
-        def st_d(i):
-            hn[i] = work.tile([P, H], BF16, name="hn")
-            nc.vector.tensor_tensor(out=hn[i][:], in0=s1[i][:], in1=h_nat[i // 2][:, i % 2, :], op=ALU.add)
+        def st_d(j):
+            hn[j] = work.tile([P, 2, H], BF16, name="hn")
+            nc.vector.tensor_tensor(out=hn[j][:], in0=s1[j][:], in1=h_nat[j][:], op=ALU.add)
 
-        def st_e(i):
-            tp_hn[i] = psum.tile([P, 2, P], F32, tag="bank", name="tp_hn")
-            transpose_words(tp_hn[i], hn[i][:])
+        def st_e(j):
+            tp_hn[j] = psum.tile([P, 2, 2, P], F32, tag="bank", name="tp_hn")
+            for ii in range(2):
+                transpose_words(tp_hn[j][:, ii], hn[j][:, ii, :])
 
-        def st_f(i):
-            half, q = i // 4, i % 4
+        def st_f(j):
+            half, q = j // 2, j % 2
             nc.scalar.copy(
-                out=hnI[half][:, q * 512 : (q + 1) * 512].bitcast(F32).rearrange("p (n u) -> p n u", u=2),
-                in_=tp_hn[i][:].rearrange("p u n -> p n u"),
+                out=hnI[half][:, q * 1024 : (q + 1) * 1024].bitcast(F32).rearrange("p (i n u) -> p i n u", i=2, u=2),
+                in_=tp_hn[j][:].rearrange("p i u n -> p i n u"),
             )
 
-        def st_g(part):
-            half, lo, hi_ = {0: (0, 0, 4), 1: (1, 0, 4), 8: (1, 0, 2), 9: (1, 2, 4)}[part]
+        def st_g(j):
+            half, q = j // 2, j % 2
             nc.vector.quantize_mx(
-                out=hn_codes[half][:, lo * P : hi_ * P].bitcast(FP8X4),
-                scales=hn_scales[half][:, lo * P : hi_ * P],
-                in_=hnI[half][:, lo * 4 * P : hi_ * 4 * P],
+                out=hn_codes[half][:, q * 2 * P : (q + 1) * 2 * P].bitcast(FP8X4),
+                scales=hn_scales[half][:, q * 2 * P : (q + 1) * 2 * P],
+                in_=hnI[half][:, q * 1024 : (q + 1) * 1024],
             )
 
         def st_h(i):
@@ -278,66 +279,55 @@ def tile_differ_amplifier_pa_kernel(tc, h, w, w_ff, b_ff, out):
         cw("wff", wff_I, 1)
         st_a(0)
         st_a(1)
-        quant_weight(w_I, w_codes, w_scales, 0)
-        quant_weight(w_I, w_codes, w_scales, 1)
+        quant_weight(w_I, w_codes, w_scales)
         st_b(0)
         st_c(0)
         st_c(1)
+        st_b(1)
         st_c(2)
         st_c(3)
         st_aV(2)
         st_d(0)
         st_e(0)
         st_f(0)
-        st_d(1)
-        st_e(1)
-        st_f(1)
-        st_aV(3)
-        st_d(2)
-        st_e(2)
-        st_f(2)
-        st_d(3)
-        st_e(3)
-        st_f(3)
+        st_b(2)
+        st_c(4)
+        st_c(5)
         bias_ps = psum.tile([P, O], F32, tag="bank", name="bias_ps")
         nc.tensor.matmul(bias_ps[:], lhsT=ones[:], rhs=brow[:], start=True, stop=True)
         nc.scalar.copy(out=biasB[:], in_=bias_ps[:])
-        st_b(1)
-        st_c(4)
-        st_c(5)
+        st_aV(3)
+        st_d(1)
+        st_e(1)
+        st_f(1)
+        st_b(3)
         st_c(6)
         st_c(7)
-        quant_weight(wff_I, wff_codes, wff_scales, 0)
-        quant_weight(wff_I, wff_codes, wff_scales, 1)
+        quant_weight(wff_I, wff_codes, wff_scales)
+        st_d(2)
+        st_e(2)
+        st_f(2)
         st_g(0)
         st_h(0)
         st_h(1)
+        st_d(3)
+        st_e(3)
+        st_f(3)
+        st_g(1)
         st_h(2)
         st_h(3)
-        st_d(4)
-        st_e(4)
-        st_f(4)
-        st_d(5)
-        st_e(5)
-        st_f(5)
-        st_d(6)
-        st_e(6)
-        st_f(6)
-        st_d(7)
-        st_e(7)
-        st_f(7)
         st_i(0)
         st_j(0)
         st_i(1)
         st_j(1)
-        st_i(2)
-        st_j(2)
-        st_g(8)
+        st_g(2)
         st_h(4)
         st_h(5)
+        st_i(2)
+        st_j(2)
         st_i(3)
         st_j(3)
-        st_g(9)
+        st_g(3)
         st_h(6)
         st_h(7)
         st_i(4)

@@ -254,6 +254,36 @@ def tile_differ_amplifier_pa_kernel(tc, h, w, w_ff, b_ff, out):
             nc.scalar.activation(out=res[i][:, lo:hi_], in_=pre[i][:, lo:hi_], func=ACT.Sigmoid)
             nc.sync.dma_start(out=out_v[:, i, lo:hi_], in_=res[i][:, lo:hi_])
 
+        s1t = [None] * 2
+        hnt = [None] * 2
+        tpt = [None] * 2
+
+        def st_ct(i):
+            s1t[i] = psum.tile([P, H], BANK1, tag="bank", name="s1t")
+            nc.tensor.matmul_mx(
+                out=s1t[i][:],
+                lhsT=r_codes[0][:, i * P : (i + 1) * P].bitcast(FP8X4),
+                lhsT_scale=r_scales[0][:, i * P : (i + 1) * P],
+                rhs=w_codes[:].bitcast(FP8X4),
+                rhs_scale=w_scales[:],
+                start=True,
+                stop=True,
+            )
+
+        def st_dt(i):
+            hnt[i] = work.tile([P, H], BF16, name="hnt")
+            nc.vector.tensor_tensor(out=hnt[i][:], in0=s1t[i][:], in1=h_nat[0][:, i, :], op=ALU.add)
+
+        def st_et(i):
+            tpt[i] = psum.tile([P, 2, P], F32, tag="bank", name="tpt")
+            transpose_words(tpt[i], hnt[i][:])
+
+        def st_ft(i):
+            nc.scalar.copy(
+                out=hnI[0][:, i * 512 : (i + 1) * 512].bitcast(F32).rearrange("p (n u) -> p n u", u=2),
+                in_=tpt[i][:].rearrange("p u n -> p n u"),
+            )
+
         warm_up(3)
         totals(0)
         th(0)
@@ -277,25 +307,28 @@ def tile_differ_amplifier_pa_kernel(tc, h, w, w_ff, b_ff, out):
         cw("wff", wff_I, 0)
         tw("wff", wff_nat, 1)
         cw("wff", wff_I, 1)
+        bias_ps = psum.tile([P, O], F32, tag="bank", name="bias_ps")
+        nc.tensor.matmul(bias_ps[:], lhsT=ones[:], rhs=brow[:], start=True, stop=True)
+        nc.scalar.copy(out=biasB[:], in_=bias_ps[:])
         st_a(0)
         st_a(1)
         quant_weight(w_I, w_codes, w_scales)
         st_b(0)
-        st_c(0)
-        st_c(1)
+        st_ct(0)
+        st_ct(1)
         st_b(1)
         st_c(2)
         st_c(3)
         st_aV(2)
-        st_d(0)
-        st_e(0)
-        st_f(0)
         st_b(2)
         st_c(4)
         st_c(5)
-        bias_ps = psum.tile([P, O], F32, tag="bank", name="bias_ps")
-        nc.tensor.matmul(bias_ps[:], lhsT=ones[:], rhs=brow[:], start=True, stop=True)
-        nc.scalar.copy(out=biasB[:], in_=bias_ps[:])
+        st_dt(0)
+        st_et(0)
+        st_ft(0)
+        st_dt(1)
+        st_et(1)
+        st_ft(1)
         st_aV(3)
         st_d(1)
         st_e(1)
@@ -304,12 +337,12 @@ def tile_differ_amplifier_pa_kernel(tc, h, w, w_ff, b_ff, out):
         st_c(6)
         st_c(7)
         quant_weight(wff_I, wff_codes, wff_scales)
-        st_d(2)
-        st_e(2)
-        st_f(2)
         st_g(0)
         st_h(0)
         st_h(1)
+        st_d(2)
+        st_e(2)
+        st_f(2)
         st_d(3)
         st_e(3)
         st_f(3)
@@ -325,11 +358,11 @@ def tile_differ_amplifier_pa_kernel(tc, h, w, w_ff, b_ff, out):
         st_h(5)
         st_i(2)
         st_j(2)
-        st_i(3)
-        st_j(3)
         st_g(3)
         st_h(6)
         st_h(7)
+        st_i(3)
+        st_j(3)
         st_i(4)
         st_j(4)
         st_i(5)

@@ -178,8 +178,8 @@ def tile_differ_amplifier_pa_kernel(tc, h, w, w_ff, b_ff, out):
 
         def st_aV(j):
             nc.vector.tensor_copy(
-                out=rI[j // 2][:, (j % 2) * 1024 : (j % 2 + 1) * 1024].rearrange("p (n t) -> p n t", t=4),
-                in_=rT[j][:].rearrange("p t i n -> p (i n) t"),
+                out=rI[j // 2][:, (j % 2) * 1024 : (j % 2 + 1) * 1024].rearrange("p (c s t) -> p c t s", s=4, t=4),
+                in_=rT[j][:].rearrange("p t i n -> p t (i n)").rearrange("p t (c s) -> p c t s", s=4),
             )
 
         def st_b(j):

@@ -248,11 +248,11 @@ def tile_differ_amplifier_pa_kernel(tc, h, w, w_ff, b_ff, out):
                 pre[i] = work.tile([P, O], F32, name="pre")
             nc.vector.tensor_tensor(out=pre[i][:, lo:hi_], in0=s2[i][:, lo:hi_], in1=biasB[:, lo:hi_], op=ALU.add)
 
-        def st_j(i, lo=0, hi_=O):
+        def st_j(i, lo=0, hi_=O, queue=None):
             if lo == 0:
                 res[i] = work.tile([P, O], F32, name="res")
             nc.scalar.activation(out=res[i][:, lo:hi_], in_=pre[i][:, lo:hi_], func=ACT.Sigmoid)
-            nc.sync.dma_start(out=out_v[:, i, lo:hi_], in_=res[i][:, lo:hi_])
+            (queue or nc.sync).dma_start(out=out_v[:, i, lo:hi_], in_=res[i][:, lo:hi_])
 
         s1t = [None] * 2
         hnt = [None] * 2
@@ -372,4 +372,4 @@ def tile_differ_amplifier_pa_kernel(tc, h, w, w_ff, b_ff, out):
         st_i(7, 0, 256)
         st_j(7, 0, 256)
         st_i(7, 256, 512)
-        st_j(7, 256, 512)
+        st_j(7, 256, 512, nc.scalar)

@@ -74,7 +74,8 @@ def tile_differ_amplifier_pa_kernel(tc, h, w, w_ff, b_ff, out):
             for u in range(2):
                 nc.tensor.transpose(bank[:, u, :], words[:, u : H // 2 : 2], ident[:])
 
-        tot_ps = psum.tile([P, 4, NT], F32, tag="bank", name="tot_ps")
+        tot_ps = psum.tile([P, 4, NT - 2], F32, tag="bank", name="tot_ps")
+        last_ps = psum.tile([P, 4], F32, tag="bank", name="last_ps")
         hI = [None] * 4
 
         def totals(j):
@@ -87,6 +88,17 @@ def tile_differ_amplifier_pa_kernel(tc, h, w, w_ff, b_ff, out):
                         rhs=ones[:, 0:1],
                         start=True,
                         stop=True,
+                    )
+
+        def totals_last():
+            for t in range(4):
+                for ii in range(2):
+                    nc.tensor.matmul(
+                        last_ps[:, t : t + 1],
+                        lhsT=h_nat[3][:, ii, t:H:4],
+                        rhs=ones[:, 0:1],
+                        start=(ii == 0),
+                        stop=(ii == 1),
                     )
 
         tp_h = [None] * 4
@@ -129,6 +141,7 @@ def tile_differ_amplifier_pa_kernel(tc, h, w, w_ff, b_ff, out):
         w_I, w_codes, w_scales = weight_tiles("w")
         wff_I, wff_codes, wff_scales = weight_tiles("wff")
         tot = const.tile([P, 4], F32, name="tot")
+        part = const.tile([P, 4], F32, name="part")
         cmean = const.tile([P, 4], F32, name="cmean")
         biasB = const.tile([P, O], F32, name="biasB")
 
@@ -290,9 +303,12 @@ def tile_differ_amplifier_pa_kernel(tc, h, w, w_ff, b_ff, out):
         hi(0)
         totals(1)
         totals(2)
-        totals(3)
         nc.vector.tensor_reduce(out=tot[:], in_=tot_ps[:], axis=AX.X, op=ALU.add)
-        nc.vector.tensor_scalar_mul(cmean[:], tot[:], -1.0 / (N_ROWS - 1))
+        nc.vector.tensor_scalar_mul(part[:], tot[:], -1.0 / (N_ROWS - 1))
+        totals_last()
+        nc.vector.scalar_tensor_tensor(
+            out=cmean[:], in0=last_ps[:], scalar=-1.0 / (N_ROWS - 1), in1=part[:], op0=ALU.mult, op1=ALU.add
+        )
         th(1)
         hi(1)
         tw("w", w_nat, 0)
@@ -326,23 +342,23 @@ def tile_differ_amplifier_pa_kernel(tc, h, w, w_ff, b_ff, out):
         st_dt(0)
         st_et(0)
         st_ft(0)
+        st_aV(3)
         st_dt(1)
         st_et(1)
         st_ft(1)
-        st_aV(3)
-        st_d(1)
-        st_e(1)
-        st_f(1)
         st_b(3)
         st_c(6)
         st_c(7)
+        st_d(1)
+        st_e(1)
+        st_f(1)
+        st_d(2)
+        st_e(2)
+        st_f(2)
         quant_weight(wff_I, wff_codes, wff_scales)
         st_g(0)
         st_h(0)
         st_h(1)
-        st_d(2)
-        st_e(2)
-        st_f(2)
         st_d(3)
         st_e(3)
         st_f(3)

@@ -218,13 +218,19 @@ def tile_differ_amplifier_pa_kernel(tc, h, w, w_ff, b_ff, out):
             )
 
         def st_d(j):
-            hn[j] = work.tile([P, 2, H], BF16, name="hn")
-            nc.vector.tensor_tensor(out=hn[j][:], in0=s1[j][:], in1=h_nat[j][:], op=ALU.add)
+            hn[j] = work.tile([P, 2, 2, H // 2], BF16, name="hn")
+            nc.vector.tensor_tensor(
+                out=hn[j][:].rearrange("p u i (w e) -> p (i w) u e", e=2),
+                in0=s1[j][:].rearrange("p i (w u e) -> p (i w) u e", u=2, e=2),
+                in1=h_nat[j][:].rearrange("p i (w u e) -> p (i w) u e", u=2, e=2),
+                op=ALU.add,
+            )
 
         def st_e(j):
             tp_hn[j] = psum.tile([P, 2, 2, P], F32, tag="bank", name="tp_hn")
             for ii in range(2):
-                transpose_words(tp_hn[j][:, ii], hn[j][:, ii, :])
+                for u in range(2):
+                    nc.tensor.transpose(tp_hn[j][:, ii, u, :], hn[j][:, u, ii, :].bitcast(F32), ident[:])
 
         def st_f(j):
             half, q = j // 2, j % 2
@@ -284,12 +290,18 @@ def tile_differ_amplifier_pa_kernel(tc, h, w, w_ff, b_ff, out):
             )
 
         def st_dt(i):
-            hnt[i] = work.tile([P, H], BF16, name="hnt")
-            nc.vector.tensor_tensor(out=hnt[i][:], in0=s1t[i][:], in1=h_nat[0][:, i, :], op=ALU.add)
+            hnt[i] = work.tile([P, 2, H // 2], BF16, name="hnt")
+            nc.vector.tensor_tensor(
+                out=hnt[i][:].rearrange("p u (w e) -> p w u e", e=2),
+                in0=s1t[i][:].rearrange("p (w u e) -> p w u e", u=2, e=2),
+                in1=h_nat[0][:, i, :].rearrange("p (w u e) -> p w u e", u=2, e=2),
+                op=ALU.add,
+            )
 
         def st_et(i):
             tpt[i] = psum.tile([P, 2, P], F32, tag="bank", name="tpt")
-            transpose_words(tpt[i], hnt[i][:])
+            for u in range(2):
+                nc.tensor.transpose(tpt[i][:, u, :], hnt[i][:, u, :].bitcast(F32), ident[:])
 
         def st_ft(i):
             nc.scalar.copy(

@@ -309,6 +309,16 @@ def tile_differ_amplifier_pa_kernel(tc, h, w, w_ff, b_ff, out):
                 in_=tpt[i][:].rearrange("p u n -> p n u"),
             )
 
+        def st_aG(j):
+            nc.gpsimd.tensor_scalar(
+                out=rI[j // 2][:, (j % 2) * 1024 : (j % 2 + 1) * 1024].rearrange("p (n t) -> p n t", t=4),
+                in0=rT[j][:].rearrange("p t i n -> p (i n) t"),
+                scalar1=1.0,
+                scalar2=0.0,
+                op0=ALU.mult,
+                op1=ALU.add,
+            )
+
         warm_up(3)
         totals(0)
         th(0)
@@ -331,6 +341,7 @@ def tile_differ_amplifier_pa_kernel(tc, h, w, w_ff, b_ff, out):
         st_aS(2)
         th(3)
         st_aS(3)
+        st_aG(3)
         tw("wff", wff_nat, 0)
         cw("wff", wff_I, 0)
         tw("wff", wff_nat, 1)
@@ -354,23 +365,22 @@ def tile_differ_amplifier_pa_kernel(tc, h, w, w_ff, b_ff, out):
         st_dt(0)
         st_et(0)
         st_ft(0)
-        st_aV(3)
         st_dt(1)
         st_et(1)
         st_ft(1)
-        st_b(3)
-        st_c(6)
-        st_c(7)
         st_d(1)
         st_e(1)
         st_f(1)
-        st_d(2)
-        st_e(2)
-        st_f(2)
+        st_b(3)
+        st_c(6)
+        st_c(7)
         quant_weight(wff_I, wff_codes, wff_scales)
         st_g(0)
         st_h(0)
         st_h(1)
+        st_d(2)
+        st_e(2)
+        st_f(2)
         st_d(3)
         st_e(3)
         st_f(3)

@@ -108,6 +108,20 @@ def tile_differ_amplifier_pa_kernel(tc, h, w, w_ff, b_ff, out):
             for ii in range(2):
                 transpose_words(tp_h[j][:, ii], h_nat[j][:, ii, :])
 
+        h_sorted = [None] * 4
+
+        def sort_words(j):
+            h_sorted[j] = keep.tile([P, 2, 2, P], F32, name="h_sorted%d" % j)
+            nc.vector.tensor_copy(
+                out=h_sorted[j][:], in_=h_nat[j][:].bitcast(F32).rearrange("p i (w u) -> p u i w", u=2)
+            )
+
+        def th_sorted(j):
+            tp_h[j] = psum.tile([P, 2, 2, P], F32, tag="bank", name="tp_h")
+            for ii in range(2):
+                for u in range(2):
+                    nc.tensor.transpose(tp_h[j][:, ii, u, :], h_sorted[j][:, u, ii, :], ident[:])
+
         def hi(j):
             hI[j] = keep.tile([P, 2 * P * 4], BF16, name="hI%d" % j, align_bytes=64)
             nc.scalar.copy(
@@ -324,22 +338,25 @@ def tile_differ_amplifier_pa_kernel(tc, h, w, w_ff, b_ff, out):
         th(0)
         hi(0)
         totals(1)
+        sort_words(1)
         totals(2)
+        sort_words(2)
+        sort_words(3)
         nc.vector.tensor_reduce(out=tot[:], in_=tot_ps[:], axis=AX.X, op=ALU.add)
         nc.vector.tensor_scalar_mul(part[:], tot[:], -1.0 / (N_ROWS - 1))
         totals_last()
         nc.vector.scalar_tensor_tensor(
             out=cmean[:], in0=last_ps[:], scalar=-1.0 / (N_ROWS - 1), in1=part[:], op0=ALU.mult, op1=ALU.add
         )
-        th(1)
+        th_sorted(1)
         hi(1)
         tw("w", w_nat, 0)
         cw("w", w_I, 0)
         tw("w", w_nat, 1)
         cw("w", w_I, 1)
-        th(2)
+        th_sorted(2)
         st_aS(2)
-        th(3)
+        th_sorted(3)
         st_aS(3)
         st_aG(3)
         tw("wff", wff_nat, 0)
@@ -371,16 +388,16 @@ def tile_differ_amplifier_pa_kernel(tc, h, w, w_ff, b_ff, out):
         st_d(1)
         st_e(1)
         st_f(1)
+        quant_weight(wff_I, wff_codes, wff_scales)
         st_b(3)
         st_c(6)
         st_c(7)
-        quant_weight(wff_I, wff_codes, wff_scales)
-        st_g(0)
-        st_h(0)
-        st_h(1)
         st_d(2)
         st_e(2)
         st_f(2)
+        st_g(0)
+        st_h(0)
+        st_h(1)
         st_d(3)
         st_e(3)
         st_f(3)

@@ -341,9 +341,9 @@ def tile_differ_amplifier_pa_kernel(tc, h, w, w_ff, b_ff, out):
         sort_words(1)
         totals(2)
         sort_words(2)
-        sort_words(3)
         nc.vector.tensor_reduce(out=tot[:], in_=tot_ps[:], axis=AX.X, op=ALU.add)
         nc.vector.tensor_scalar_mul(part[:], tot[:], -1.0 / (N_ROWS - 1))
+        sort_words(3)
         totals_last()
         nc.vector.scalar_tensor_tensor(
             out=cmean[:], in0=last_ps[:], scalar=-1.0 / (N_ROWS - 1), in1=part[:], op0=ALU.mult, op1=ALU.add
@@ -372,10 +372,10 @@ def tile_differ_amplifier_pa_kernel(tc, h, w, w_ff, b_ff, out):
         st_b(0)
         st_ct(0)
         st_ct(1)
+        st_aV(2)
         st_b(1)
         st_c(2)
         st_c(3)
-        st_aV(2)
         st_b(2)
         st_c(4)
         st_c(5)

@@ -18,6 +18,7 @@ AX = mybir.AxisListType
 P = 128
 NT = N_ROWS // P
 BANK1 = BF16
+SUM_N = 54
 
 
 def tile_differ_amplifier_pa_kernel(tc, h, w, w_ff, b_ff, out):
@@ -56,9 +57,8 @@ def tile_differ_amplifier_pa_kernel(tc, h, w, w_ff, b_ff, out):
         nc.vector.memset(junk[:], 0.0)
         ident = const.tile([P, P], F32, name="ident")
         make_identity(nc, ident[:])
-        brow = const.tile([P, O], BF16, name="brow")
-        nc.vector.memset(brow[:], 0.0)
-        nc.scalar.dma_start(out=brow[0:1, :], in_=b_ff.rearrange("(a o) -> a o", a=1))
+        biasB = const.tile([P, O], BF16, name="biasB")
+        nc.sync.dma_start(out=biasB[:], in_=b_ff.partition_broadcast(P))
         warm = const.tile([P, 1], F32, name="warm")
         nc.vector.memset(warm[:], 0.0)
         nc.scalar.activation(out=warm[:], in_=warm[:], func=ACT.Sigmoid)
@@ -74,8 +74,8 @@ def tile_differ_amplifier_pa_kernel(tc, h, w, w_ff, b_ff, out):
             for u in range(2):
                 nc.tensor.transpose(bank[:, u, :], words[:, u : H // 2 : 2], ident[:])
 
-        tot_ps = psum.tile([P, 4, NT - 2], F32, tag="bank", name="tot_ps")
-        last_ps = psum.tile([P, 4], F32, tag="bank", name="last_ps")
+        tot_ps = psum.tile([P, 4 * (NT - 2) + SUM_N], F32, tag="bank", name="tot_ps")
+        last_ps = psum.tile([P, 4 + SUM_N], F32, tag="bank", name="last_ps")
         hI = [None] * 4
 
         def totals(j):
@@ -83,9 +83,9 @@ def tile_differ_amplifier_pa_kernel(tc, h, w, w_ff, b_ff, out):
                 i = 2 * j + ii
                 for t in range(4):
                     nc.tensor.matmul(
-                        tot_ps[:, t, i : i + 1],
+                        tot_ps[:, 4 * i + t : 4 * i + t + SUM_N],
                         lhsT=h_nat[j][:, ii, t:H:4],
-                        rhs=ones[:, 0:1],
+                        rhs=ones[:, 0:SUM_N],
                         start=True,
                         stop=True,
                     )
@@ -94,9 +94,9 @@ def tile_differ_amplifier_pa_kernel(tc, h, w, w_ff, b_ff, out):
             for t in range(4):
                 for ii in range(2):
                     nc.tensor.matmul(
-                        last_ps[:, t : t + 1],
+                        last_ps[:, t : t + SUM_N],
                         lhsT=h_nat[3][:, ii, t:H:4],
-                        rhs=ones[:, 0:1],
+                        rhs=ones[:, 0:SUM_N],
                         start=(ii == 0),
                         stop=(ii == 1),
                     )
@@ -157,7 +157,6 @@ def tile_differ_amplifier_pa_kernel(tc, h, w, w_ff, b_ff, out):
         tot = const.tile([P, 4], F32, name="tot")
         part = const.tile([P, 4], F32, name="part")
         cmean = const.tile([P, 4], F32, name="cmean")
-        biasB = const.tile([P, O], F32, name="biasB")
 
         rI = []
         r_codes = []
@@ -341,12 +340,14 @@ def tile_differ_amplifier_pa_kernel(tc, h, w, w_ff, b_ff, out):
         sort_words(1)
         totals(2)
         sort_words(2)
-        nc.vector.tensor_reduce(out=tot[:], in_=tot_ps[:], axis=AX.X, op=ALU.add)
+        nc.vector.tensor_reduce(
+            out=tot[:], in_=tot_ps[:, 0 : 4 * (NT - 2)].rearrange("p (i t) -> p t i", t=4), axis=AX.X, op=ALU.add
+        )
         nc.vector.tensor_scalar_mul(part[:], tot[:], -1.0 / (N_ROWS - 1))
         sort_words(3)
         totals_last()
         nc.vector.scalar_tensor_tensor(
-            out=cmean[:], in0=last_ps[:], scalar=-1.0 / (N_ROWS - 1), in1=part[:], op0=ALU.mult, op1=ALU.add
+            out=cmean[:], in0=last_ps[:, 0:4], scalar=-1.0 / (N_ROWS - 1), in1=part[:], op0=ALU.mult, op1=ALU.add
         )
         th_sorted(1)
         hi(1)
@@ -363,9 +364,6 @@ def tile_differ_amplifier_pa_kernel(tc, h, w, w_ff, b_ff, out):
         cw("wff", wff_I, 0)
         tw("wff", wff_nat, 1)
         cw("wff", wff_I, 1)
-        bias_ps = psum.tile([P, O], F32, tag="bank", name="bias_ps")
-        nc.tensor.matmul(bias_ps[:], lhsT=ones[:], rhs=brow[:], start=True, stop=True)
-        nc.scalar.copy(out=biasB[:], in_=bias_ps[:])
         st_a(0)
         st_a(1)
         quant_weight(w_I, w_codes, w_scales)

@@ -332,7 +332,7 @@ def tile_differ_amplifier_pa_kernel(tc, h, w, w_ff, b_ff, out):
                 op1=ALU.add,
             )
 
-        warm_up(3)
+        warm_up(2)
         totals(0)
         th(0)
         hi(0)
@@ -355,6 +355,7 @@ def tile_differ_amplifier_pa_kernel(tc, h, w, w_ff, b_ff, out):
         cw("w", w_I, 0)
         tw("w", w_nat, 1)
         cw("w", w_I, 1)
+        warm_up(1)
         th_sorted(2)
         st_aS(2)
         th_sorted(3)

from contextlib import ExitStack

import concourse.mybir as mybir
from concourse.masks import make_identity

N_ROWS, H, O = 1024, 512, 512
FLOPS = 2 * N_ROWS * H * H + 2 * N_ROWS * H * O

F32 = mybir.dt.float32
BF16 = mybir.dt.bfloat16
U32 = mybir.dt.uint32
U8 = mybir.dt.uint8
FP8X4 = mybir.dt.float8_e4m3fn_x4
ALU = mybir.AluOpType
ACT = mybir.ActivationFunctionType
AX = mybir.AxisListType

P = 128
NT = N_ROWS // P
BANK1 = BF16
SUM_N = 54


def tile_differ_amplifier_pa_kernel(tc, h, w, w_ff, b_ff, out):
    nc = tc.nc
    with ExitStack() as ctx:
        const = ctx.enter_context(tc.tile_pool(name="const", bufs=1))
        keep = ctx.enter_context(tc.tile_pool(name="keep", bufs=1))
        work = ctx.enter_context(tc.tile_pool(name="work", bufs=8))
        psum = ctx.enter_context(tc.psum_pool(name="psum", bufs=8))
        ctx.enter_context(tc.manual_schedule())

        h_v = h.rearrange("(p i) k -> p i k", i=NT)
        out_v = out.rearrange("(p i) o -> p i o", i=NT)
        w_v = w.rearrange("(j m) k -> m j k", j=4)
        wff_v = w_ff.rearrange("(j m) k -> m j k", j=4)

        h_nat = []
        for j in range(4):
            t = keep.tile([P, 2, H], BF16, name="h_nat%d" % j)
            nc.sync.dma_start(out=t[:], in_=h_v[:, 2 * j : 2 * j + 2, :])
            h_nat.append(t)
        w_nat = []
        for b in range(2):
            t = keep.tile([P, 2, H], BF16, name="w_nat%d" % b)
            nc.sync.dma_start(out=t[:], in_=w_v[:, 2 * b : 2 * b + 2, :])
            w_nat.append(t)
        wff_nat = []
        for b in range(2):
            t = keep.tile([P, 2, H], BF16, name="wff_nat%d" % b)
            nc.sync.dma_start(out=t[:], in_=wff_v[:, 2 * b : 2 * b + 2, :])
            wff_nat.append(t)

        ones = const.tile([P, P], BF16, name="ones")
        nc.vector.memset(ones[:], 1.0)
        junk = const.tile([P, O], BF16, name="junk")
        nc.vector.memset(junk[:], 0.0)
        ident = const.tile([P, P], F32, name="ident")
        make_identity(nc, ident[:])
        biasB = const.tile([P, O], BF16, name="biasB")
        nc.sync.dma_start(out=biasB[:], in_=b_ff.partition_broadcast(P))
        warm = const.tile([P, 1], F32, name="warm")
        nc.vector.memset(warm[:], 0.0)
        nc.scalar.activation(out=warm[:], in_=warm[:], func=ACT.Sigmoid)

        warm_ps = psum.tile([P, O], F32, tag="bank", name="warm_ps")

        def warm_up(count):
            for rep in range(count):
                nc.tensor.matmul(warm_ps[:], lhsT=ones[:], rhs=junk[:], start=True, stop=True)

        def transpose_words(bank, src_bf16):
            words = src_bf16.bitcast(F32)
            for u in range(2):
                nc.tensor.transpose(bank[:, u, :], words[:, u : H // 2 : 2], ident[:])

        tot_ps = psum.tile([P, 4 * (NT - 2) + SUM_N], F32, tag="bank", name="tot_ps")
        last_ps = psum.tile([P, 4 + SUM_N], F32, tag="bank", name="last_ps")
        hI = [None] * 4

        def totals(j):
            for ii in range(2):
                i = 2 * j + ii
                for t in range(4):
                    nc.tensor.matmul(
                        tot_ps[:, 4 * i + t : 4 * i + t + SUM_N],
                        lhsT=h_nat[j][:, ii, t:H:4],
                        rhs=ones[:, 0:SUM_N],
                        start=True,
                        stop=True,
                    )

        def totals_last():
            for t in range(4):
                for ii in range(2):
                    nc.tensor.matmul(
                        last_ps[:, t : t + SUM_N],
                        lhsT=h_nat[3][:, ii, t:H:4],
                        rhs=ones[:, 0:SUM_N],
                        start=(ii == 0),
                        stop=(ii == 1),
                    )

        tp_h = [None] * 4

        def th(j):
            tp_h[j] = psum.tile([P, 2, 2, P], F32, tag="bank", name="tp_h")
            for ii in range(2):
                transpose_words(tp_h[j][:, ii], h_nat[j][:, ii, :])

        h_sorted = [None] * 4

        def sort_words(j):
            h_sorted[j] = keep.tile([P, 2, 2, P], F32, name="h_sorted%d" % j)
            nc.vector.tensor_copy(
                out=h_sorted[j][:], in_=h_nat[j][:].bitcast(F32).rearrange("p i (w u) -> p u i w", u=2)
            )

        def th_sorted(j):
            tp_h[j] = psum.tile([P, 2, 2, P], F32, tag="bank", name="tp_h")
            for ii in range(2):
                for u in range(2):
                    nc.tensor.transpose(tp_h[j][:, ii, u, :], h_sorted[j][:, u, ii, :], ident[:])

        def hi(j):
            hI[j] = keep.tile([P, 2 * P * 4], BF16, name="hI%d" % j, align_bytes=64)
            nc.scalar.copy(
                out=hI[j][:].bitcast(F32).rearrange("p (i n u) -> p i n u", i=2, u=2),
                in_=tp_h[j][:].rearrange("p i u n -> p i n u"),
            )

        def weight_tiles(label):
            grouped = keep.tile([P, O * 4], BF16, name=label + "_I", align_bytes=64)
            codes = keep.tile([P, O], U32, name=label + "_codes", align_bytes=64)
            scales = keep.tile([P, O], U8, name=label + "_scales", align_bytes=64)
            return grouped, codes, scales

        tp_w = {}

        def tw(label, nat, b):
            tp_w[(label, b)] = psum.tile([P, 2, 2, P], F32, tag="bank", name="tp_w")
            for jj in range(2):
                transpose_words(tp_w[(label, b)][:, jj], nat[b][:, jj, :])

        def cw(label, grouped, b):
            dst = grouped[:, b * 1024 : (b + 1) * 1024].bitcast(F32)
            nc.scalar.copy(
                out=dst.rearrange("p (j m u) -> p j m u", j=2, u=2),
                in_=tp_w[(label, b)][:].rearrange("p j u m -> p j m u"),
            )

        def quant_weight(grouped, codes, scales):
            nc.vector.quantize_mx(out=codes[:].bitcast(FP8X4), scales=scales[:], in_=grouped[:])

        w_I, w_codes, w_scales = weight_tiles("w")
        wff_I, wff_codes, wff_scales = weight_tiles("wff")
        tot = const.tile([P, 4], F32, name="tot")
        part = const.tile([P, 4], F32, name="part")
        cmean = const.tile([P, 4], F32, name="cmean")

        rI = []
        r_codes = []
        r_scales = []
        hnI = []
        hn_codes = []
        hn_scales = []
        for half in range(2):
            rI.append(keep.tile([P, 2048], BF16, name="rI%d" % half, align_bytes=64))
            r_codes.append(keep.tile([P, 512], U32, name="r_codes%d" % half, align_bytes=64))
            r_scales.append(keep.tile([P, 512], U8, name="r_scales%d" % half, align_bytes=64))
            hnI.append(keep.tile([P, 2048], BF16, name="hnI%d" % half, align_bytes=64))
            hn_codes.append(keep.tile([P, 512], U32, name="hn_codes%d" % half, align_bytes=64))
            hn_scales.append(keep.tile([P, 512], U8, name="hn_scales%d" % half, align_bytes=64))
        s1 = [None] * 4
        hn = [None] * 4
        tp_hn = [None] * 4
        s2 = [None] * NT
        pre = [None] * NT

        def st_a(j):
            nc.vector.scalar_tensor_tensor(
                out=rI[j // 2][:, (j % 2) * 1024 : (j % 2 + 1) * 1024].rearrange("p (n t) -> p n t", t=4),
                in0=hI[j][:].rearrange("p (n t) -> p n t", t=4),
                scalar=float(N_ROWS) / (N_ROWS - 1),
                in1=cmean[:].unsqueeze(1).to_broadcast([P, 2 * P, 4]),
                op0=ALU.mult,
                op1=ALU.add,
            )

        rT = [None] * 4

        def st_aS(j):
            rT[j] = keep.tile([P, 4, 2, P], BF16, name="rT%d" % j)
            halves = tp_h[j][:].bitcast(BF16).rearrange("p i u (n e) -> p i u n e", e=2)
            for u in range(2):
                for e in range(2):
                    nc.scalar.activation(
                        out=rT[j][:, 2 * u + e],
                        in_=halves[:, :, u, :, e],
                        func=ACT.Identity,
                        scale=float(N_ROWS) / (N_ROWS - 1),
                        bias=cmean[:, 2 * u + e : 2 * u + e + 1],
                    )

        def st_aV(j):
            nc.vector.tensor_copy(
                out=rI[j // 2][:, (j % 2) * 1024 : (j % 2 + 1) * 1024].rearrange("p (c s t) -> p c t s", s=4, t=4),
                in_=rT[j][:].rearrange("p t i n -> p t (i n)").rearrange("p t (c s) -> p c t s", s=4),
            )

        def st_b(j):
            half, q = j // 2, j % 2
            nc.vector.quantize_mx(
                out=r_codes[half][:, q * 2 * P : (q + 1) * 2 * P].bitcast(FP8X4),
                scales=r_scales[half][:, q * 2 * P : (q + 1) * 2 * P],
                in_=rI[half][:, q * 1024 : (q + 1) * 1024],
            )

        def st_c(i):
            half, q = i // 4, i % 4
            if i % 2 == 0:
                s1[i // 2] = psum.tile([P, 2, H], BANK1, tag="bank", name="s1")
            nc.tensor.matmul_mx(
                out=s1[i // 2][:, i % 2, :],
                lhsT=r_codes[half][:, q * P : (q + 1) * P].bitcast(FP8X4),
                lhsT_scale=r_scales[half][:, q * P : (q + 1) * P],
                rhs=w_codes[:].bitcast(FP8X4),
                rhs_scale=w_scales[:],
                start=True,
                stop=True,
            )

        def st_d(j):
            hn[j] = work.tile([P, 2, 2, H // 2], BF16, name="hn")
            nc.vector.tensor_tensor(
                out=hn[j][:].rearrange("p u i (w e) -> p (i w) u e", e=2),
                in0=s1[j][:].rearrange("p i (w u e) -> p (i w) u e", u=2, e=2),
                in1=h_nat[j][:].rearrange("p i (w u e) -> p (i w) u e", u=2, e=2),
                op=ALU.add,
            )

        def st_e(j):
            tp_hn[j] = psum.tile([P, 2, 2, P], F32, tag="bank", name="tp_hn")
            for ii in range(2):
                for u in range(2):
                    nc.tensor.transpose(tp_hn[j][:, ii, u, :], hn[j][:, u, ii, :].bitcast(F32), ident[:])

        def st_f(j):
            half, q = j // 2, j % 2
            nc.scalar.copy(
                out=hnI[half][:, q * 1024 : (q + 1) * 1024].bitcast(F32).rearrange("p (i n u) -> p i n u", i=2, u=2),
                in_=tp_hn[j][:].rearrange("p i u n -> p i n u"),
            )

        def st_g(j):
            half, q = j // 2, j % 2
            nc.vector.quantize_mx(
                out=hn_codes[half][:, q * 2 * P : (q + 1) * 2 * P].bitcast(FP8X4),
                scales=hn_scales[half][:, q * 2 * P : (q + 1) * 2 * P],
                in_=hnI[half][:, q * 1024 : (q + 1) * 1024],
            )

        def st_h(i):
            half, q = i // 4, i % 4
            s2[i] = psum.tile([P, O], F32, tag="bank", name="s2")
            nc.tensor.matmul_mx(
                out=s2[i][:],
                lhsT=hn_codes[half][:, q * P : (q + 1) * P].bitcast(FP8X4),
                lhsT_scale=hn_scales[half][:, q * P : (q + 1) * P],
                rhs=wff_codes[:].bitcast(FP8X4),
                rhs_scale=wff_scales[:],
                start=True,
                stop=True,
            )

        res = [None] * NT

        def st_i(i, lo=0, hi_=O):
            if lo == 0:
                pre[i] = work.tile([P, O], F32, name="pre")
            nc.vector.tensor_tensor(out=pre[i][:, lo:hi_], in0=s2[i][:, lo:hi_], in1=biasB[:, lo:hi_], op=ALU.add)

        def st_j(i, lo=0, hi_=O, queue=None):
            if lo == 0:
                res[i] = work.tile([P, O], F32, name="res")
            nc.scalar.activation(out=res[i][:, lo:hi_], in_=pre[i][:, lo:hi_], func=ACT.Sigmoid)
            (queue or nc.sync).dma_start(out=out_v[:, i, lo:hi_], in_=res[i][:, lo:hi_])

        s1t = [None] * 2
        hnt = [None] * 2
        tpt = [None] * 2

        def st_ct(i):
            s1t[i] = psum.tile([P, H], BANK1, tag="bank", name="s1t")
            nc.tensor.matmul_mx(
                out=s1t[i][:],
                lhsT=r_codes[0][:, i * P : (i + 1) * P].bitcast(FP8X4),
                lhsT_scale=r_scales[0][:, i * P : (i + 1) * P],
                rhs=w_codes[:].bitcast(FP8X4),
                rhs_scale=w_scales[:],
                start=True,
                stop=True,
            )

        def st_dt(i):
            hnt[i] = work.tile([P, 2, H // 2], BF16, name="hnt")
            nc.vector.tensor_tensor(
                out=hnt[i][:].rearrange("p u (w e) -> p w u e", e=2),
                in0=s1t[i][:].rearrange("p (w u e) -> p w u e", u=2, e=2),
                in1=h_nat[0][:, i, :].rearrange("p (w u e) -> p w u e", u=2, e=2),
                op=ALU.add,
            )

        def st_et(i):
            tpt[i] = psum.tile([P, 2, P], F32, tag="bank", name="tpt")
            for u in range(2):
                nc.tensor.transpose(tpt[i][:, u, :], hnt[i][:, u, :].bitcast(F32), ident[:])

        def st_ft(i):
            nc.scalar.copy(
                out=hnI[0][:, i * 512 : (i + 1) * 512].bitcast(F32).rearrange("p (n u) -> p n u", u=2),
                in_=tpt[i][:].rearrange("p u n -> p n u"),
            )

        def st_aG(j):
            nc.gpsimd.tensor_scalar(
                out=rI[j // 2][:, (j % 2) * 1024 : (j % 2 + 1) * 1024].rearrange("p (n t) -> p n t", t=4),
                in0=rT[j][:].rearrange("p t i n -> p (i n) t"),
                scalar1=1.0,
                scalar2=0.0,
                op0=ALU.mult,
                op1=ALU.add,
            )

        warm_up(2)
        totals(0)
        th(0)
        hi(0)
        totals(1)
        sort_words(1)
        totals(2)
        sort_words(2)
        nc.vector.tensor_reduce(
            out=tot[:], in_=tot_ps[:, 0 : 4 * (NT - 2)].rearrange("p (i t) -> p t i", t=4), axis=AX.X, op=ALU.add
        )
        nc.vector.tensor_scalar_mul(part[:], tot[:], -1.0 / (N_ROWS - 1))
        sort_words(3)
        totals_last()
        nc.vector.scalar_tensor_tensor(
            out=cmean[:], in0=last_ps[:, 0:4], scalar=-1.0 / (N_ROWS - 1), in1=part[:], op0=ALU.mult, op1=ALU.add
        )
        th_sorted(1)
        hi(1)
        tw("w", w_nat, 0)
        cw("w", w_I, 0)
        tw("w", w_nat, 1)
        cw("w", w_I, 1)
        warm_up(1)
        th_sorted(2)
        st_aS(2)
        th_sorted(3)
        st_aS(3)
        st_aG(3)
        tw("wff", wff_nat, 0)
        cw("wff", wff_I, 0)
        tw("wff", wff_nat, 1)
        cw("wff", wff_I, 1)
        st_a(0)
        st_a(1)
        quant_weight(w_I, w_codes, w_scales)
        st_b(0)
        st_ct(0)
        st_ct(1)
        st_aV(2)
        st_b(1)
        st_c(2)
        st_c(3)
        st_b(2)
        st_c(4)
        st_c(5)
        st_dt(0)
        st_et(0)
        st_ft(0)
        st_dt(1)
        st_et(1)
        st_ft(1)
        st_d(1)
        st_e(1)
        st_f(1)
        quant_weight(wff_I, wff_codes, wff_scales)
        st_b(3)
        st_c(6)
        st_c(7)
        st_d(2)
        st_e(2)
        st_f(2)
        st_g(0)
        st_h(0)
        st_h(1)
        st_d(3)
        st_e(3)
        st_f(3)
        st_g(1)
        st_h(2)
        st_h(3)
        st_i(0)
        st_j(0)
        st_i(1)
        st_j(1)
        st_g(2)
        st_h(4)
        st_h(5)
        st_i(2)
        st_j(2)
        st_g(3)
        st_h(6)
        st_h(7)
        st_i(3)
        st_j(3)
        st_i(4)
        st_j(4)
        st_i(5)
        st_j(5)
        st_i(6)
        st_j(6)
        st_i(7, 0, 256)
        st_j(7, 0, 256)
        st_i(7, 256, 512)
        st_j(7, 256, 512, nc.scalar)
